import numpy as np
import ml_dtypes


def mxq(x, axis, fmt="e4m3"):
    dtype, down = {"e4m3": (ml_dtypes.float8_e4m3fn, 7), "e5m2": (ml_dtypes.float8_e5m2, 14)}[fmt]
    v = np.moveaxis(np.asarray(x, np.float32).astype(ml_dtypes.bfloat16).astype(np.float64), axis, -1)
    blocks = v.reshape(v.shape[:-1] + (-1, 32))
    amax = np.abs(blocks).max(-1, keepdims=True)
    byte = np.maximum(np.where(amax > 0, np.frexp(amax)[1] - 1 + 127, 0) - down, 1)
    scale = np.exp2(byte - 127.0)
    codes = (blocks / scale).astype(np.float32).astype(dtype).astype(np.float64)
    return np.moveaxis((codes * scale).reshape(v.shape), -1, axis)


WIDE = False


def mx_kscale(k):
    if not WIDE:
        return np.ones(k)
    levels = np.array([10, -10, 5, -5, 0])
    if k % 512:
        return np.exp2(np.random.permutation(np.resize(levels, k // 32))).repeat(32)
    a = np.empty((k // 512, 16))
    for p in range(k // 512):
        a[p, :8] = np.random.permutation(np.resize(levels, 8))
        for g in range(8):
            far = levels[np.abs(levels - a[p, g]) >= 10]
            a[p, g + 8] = far[np.random.randint(len(far))]
    return np.exp2(a.ravel()).repeat(32)


BF16 = ml_dtypes.bfloat16


def bf(x):
    return np.asarray(x, np.float32).astype(BF16)


def f64(x):
    return np.asarray(x).astype(np.float64)


B, T, D, H, HKV, DH, W = 1, 2048, 1024, 8, 2, 128, 512
HALF = DH // 2


def rope(u, sin, cos):
    p = u.reshape(u.shape[:3] + (HALF, 2))
    u1, u2 = p[..., 0], p[..., 1]
    s, c = sin[None, :, None, :], cos[None, :, None, :]
    return np.stack((u1 * c - u2 * s, u1 * s + u2 * c), axis=-1).reshape(u.shape)


def draw0():
    s = mx_kscale(D)
    inv_freq = 1.0 / (10000.0 ** (np.arange(HALF) / HALF))
    ang = np.arange(T)[:, None] * inv_freq[None, :]
    return {"x": bf(np.random.standard_normal((B, T, D)) * s),
            "Wq": bf(np.random.standard_normal((D, H * DH)) * 1.5 / np.sqrt(D) / s[:, None]),
            "Wk": bf(np.random.standard_normal((D, HKV * DH)) * 1.5 / np.sqrt(D) / s[:, None]),
            "Wv": bf(np.random.standard_normal((D, HKV * DH)) * 1.5 / np.sqrt(D) / s[:, None]),
            "rope_sin": bf(np.sin(ang)), "rope_cos": bf(np.cos(ang))}


def core(x, Wq, Wk, Wv, rope_sin, rope_cos):
    xq = mxq(f64(x), 2, "e4m3")
    q = (xq @ mxq(f64(Wq), 0, "e4m3")).reshape(B, T, H, DH)
    k = (xq @ mxq(f64(Wk), 0, "e4m3")).reshape(B, T, HKV, DH)
    v = (xq @ mxq(f64(Wv), 0, "e4m3")).reshape(B, T, HKV, DH)
    q = rope(q, f64(rope_sin), f64(rope_cos))
    k = rope(k, f64(rope_sin), f64(rope_cos))
    return q.transpose(0, 2, 1, 3), k.transpose(0, 2, 1, 3), v.transpose(0, 2, 1, 3)


def e4m3fn_bytes(y):
    return np.clip(np.asarray(y, np.float64), -448.0, 448.0).astype(np.float32).astype(ml_dtypes.float8_e4m3fn).view(np.uint8)


def e4m3fn_values(b):
    return np.asarray(b, np.uint8).view(ml_dtypes.float8_e4m3fn).astype(np.float64)


def setup_inputs():
    d = draw0()
    x0 = np.asarray(d['x']).astype(np.float64)
    s = (np.max(np.abs(x0), axis=(0, 1), keepdims=True) / 448.0).astype(np.float32)
    out = {}
    for k, v in d.items():
        if k == 'x':
            out['x_bytes'] = e4m3fn_bytes(x0 / s.astype(np.float64))
            out['x_scale'] = s
        else:
            out[k] = v
    return out


def reference(x_bytes, x_scale, Wq, Wk, Wv, rope_sin, rope_cos):
    return core(e4m3fn_values(x_bytes) * x_scale.astype(np.float64), Wq, Wk, Wv, rope_sin, rope_cos)

@@ -1,0 +1,356 @@
+from contextlib import ExitStack
+
+import concourse.masks as masks
+import concourse.mybir as mybir
+
+F32 = mybir.dt.float32
+BF16 = mybir.dt.bfloat16
+U32 = mybir.dt.uint32
+U8 = mybir.dt.uint8
+FP8 = mybir.dt.float8_e4m3fn
+FP8X4 = mybir.dt.float8_e4m3fn_x4
+MULT = mybir.AluOpType.mult
+ADD = mybir.AluOpType.add
+COPY = mybir.ActivationFunctionType.Copy
+
+T, D, DH = 2048, 1024, 128
+FLOPS = 2 * T * D * 1536
+
+P = 128
+NB = 8
+NJ = 2
+NG = 2
+NC = 3
+LOOK = 3
+V_ADD = ((7, 1, 1), (7, 2, 0))
+
+
+def tile_gqamultiheadattention_pa_kernel(
+    tc, x_bytes, x_scale, Wq, Wk, Wv, rope_sin, rope_cos, out_0, out_1, out_2
+):
+    nc = tc.nc
+    with ExitStack() as ctx:
+        keep = ctx.enter_context(tc.tile_pool(name="keep", bufs=1))
+        work = ctx.enter_context(tc.tile_pool(name="work", bufs=2))
+        psum = ctx.enter_context(tc.psum_pool(name="psum", bufs=2))
+        ctx.enter_context(tc.manual_schedule())
+
+        xb_view = x_bytes[0].rearrange("(b p j) k -> b p (j k)", p=P, j=NJ)
+        sc_view = x_scale[0, 0].rearrange("(g p t) -> p g t", p=P, t=4)
+        wq_view = Wq.rearrange("(g p j) n -> g p j n", p=P, j=4)
+        wk_view = Wk.rearrange("(g p j) n -> g p j n", p=P, j=4)
+        wv_view = Wv.rearrange("(g p j) n -> g p j n", p=P, j=4)
+        sin_view = rope_sin.rearrange("(b p j) i -> p b (j i)", p=P, j=NJ)
+        cos_view = rope_cos.rearrange("(b p j) i -> p b (j i)", p=P, j=NJ)
+        q_view = out_0[0].rearrange("h (b p j) d -> b p h (j d)", p=P, j=NJ)
+        k_view = out_1[0].rearrange("h (b p j) d -> b p h (j d)", p=P, j=NJ)
+        v_view = out_2[0].rearrange("h (b p j) d -> b p h (j d)", p=P, j=NJ)
+
+        xbytes = [keep.tile([P, NJ * D], U8, name="xbytes%d" % m) for m in range(NB)]
+        sc4 = keep.tile([P, NG, 4], F32, name="sc4")
+        wraw = {}
+        for c in range(NC):
+            for g in range(NG):
+                wraw[(g, c)] = keep.tile([P, 4, 512], BF16, name="wraw%d%d" % (g, c))
+        wgrp = [keep.tile([P, NG, 512, 4], BF16, name="wgrp%d" % c, align_bytes=64) for c in range(NC)]
+        wcodes = [keep.tile([P, NG, 512], U32, name="wcodes%d" % c, align_bytes=64) for c in range(NC)]
+        wscales = [keep.tile([P, NG, 512], U8, name="wscales%d" % c, align_bytes=64) for c in range(NC)]
+        xgrp = [keep.tile([P, NG * NJ * P * 4], BF16, name="xgrp%d" % m, align_bytes=64) for m in range(NB)]
+        xcodes = [keep.tile([P, NG * NJ * P], U32, name="xcodes%d" % m, align_bytes=64) for m in range(NB)]
+        xscales = [keep.tile([P, NG * NJ * P], U8, name="xscales%d" % m, align_bytes=64) for m in range(NB)]
+        sin_t = keep.tile([P, NB, NJ * 64], BF16, name="sin_t")
+        cos_t = keep.tile([P, NB, NJ * 64], BF16, name="cos_t")
+        sin2 = keep.tile([P, NB, NJ * 64, 2], BF16, name="sin2")
+        sgn = keep.tile([P, 2], BF16, name="sgn")
+        ident = keep.tile([P, P], F32, name="ident")
+        warm_in = keep.tile([P, 1], F32, name="warm_in")
+        warm_out = keep.tile([P, 1], F32, name="warm_out")
+
+        nc.sync.dma_start(out=xbytes[0][:], in_=xb_view[0])
+        nc.sync.dma_start(out=sin_t[:], in_=sin_view)
+        nc.sync.dma_start(out=sc4[:], in_=sc_view)
+        nc.sync.dma_start(out=xbytes[1][:], in_=xb_view[1])
+        for g in range(NG):
+            nc.sync.dma_start(out=wraw[(g, 0)][:], in_=wq_view[g][:, :, 0:512])
+        nc.sync.dma_start(out=cos_t[:], in_=cos_view)
+        for g in range(NG):
+            nc.sync.dma_start(out=wraw[(g, 1)][:], in_=wq_view[g][:, :, 512:1024])
+        nc.sync.dma_start(out=xbytes[2][:], in_=xb_view[2])
+        for g in range(NG):
+            nc.sync.dma_start(out=wraw[(g, 2)][:, :, 0:256], in_=wk_view[g])
+            nc.sync.dma_start(out=wraw[(g, 2)][:, :, 256:512], in_=wv_view[g])
+        for m in range(3, NB):
+            nc.sync.dma_start(out=xbytes[m][:], in_=xb_view[m])
+
+        nc.vector.memset(warm_in[:], 0.0)
+        nc.vector.memset(sgn[:, 0:1], -1.0)
+        nc.vector.memset(sgn[:, 1:2], 1.0)
+        nc.scalar.copy(out=warm_out[:], in_=warm_in[:])
+        masks.make_identity(nc, ident[:])
+
+        state = {}
+
+        def w_interleave(c, g, eng):
+            dst = wgrp[c][:, g, :, :]
+            src = wraw[(g, c)][:].rearrange("p j n -> p n j")
+            if eng == "g":
+                nc.gpsimd.tensor_scalar(out=dst, in0=src, scalar1=1.0, scalar2=0.0, op0=MULT, op1=ADD)
+            else:
+                nc.scalar.copy(out=dst, in_=src)
+
+        def w_quant(c):
+            nc.vector.quantize_mx(
+                out=wcodes[c][:].rearrange("p g n -> p (g n)").bitcast(FP8X4),
+                scales=wscales[c][:].rearrange("p g n -> p (g n)"),
+                in_=wgrp[c][:].rearrange("p g n j -> p (g n j)"),
+            )
+
+        def sin2_build():
+            n = NB * NJ * 64
+            nc.vector.tensor_tensor(
+                out=sin2[:].rearrange("p b n e -> p (b n) e"),
+                in0=sin_t[:].rearrange("p b n -> p (b n)").unsqueeze(2).to_broadcast([P, n, 2]),
+                in1=sgn[:].unsqueeze(1).to_broadcast([P, n, 2]),
+                op=MULT,
+            )
+
+        def x_cast(m, j, first=0, last=D):
+            if first == 0:
+                state[("xbf", m, j)] = work.tile([P, D], BF16, name="xbf", tag="xbf", bufs=6, align_bytes=64)
+            nc.scalar.copy(
+                out=state[("xbf", m, j)][:, first:last], in_=xbytes[m][:, j * D + first : j * D + last].bitcast(FP8)
+            )
+
+        def x_transpose(m):
+            for g in range(NG):
+                xt = psum.tile([P, 512], F32, name="xt", tag="xt", bufs=2)
+                for u in range(2):
+                    for j in range(NJ):
+                        s = 2 * u + j
+                        words = state[("xbf", m, j)][:].bitcast(F32)
+                        nc.tensor.transpose(
+                            xt[:, s * P : (s + 1) * P], words[:, 256 * g + u : 256 * (g + 1) : 2], ident[:]
+                        )
+                state[("xt", m, g)] = xt
+
+        def x_scale_v(m, g):
+            xt = state[("xt", m, g)]
+            nc.vector.tensor_tensor(
+                out=xgrp[m][:, g * 1024 : (g + 1) * 1024].rearrange("p (n u e) -> p n u e", u=2, e=2),
+                in0=xt[:].bitcast(BF16).rearrange("p (u n e) -> p n u e", u=2, e=2),
+                in1=sc4[:, g, :].rearrange("p (u e) -> p u e", e=2).unsqueeze(1).to_broadcast([P, 256, 2, 2]),
+                op=MULT,
+            )
+
+        def x_planes(m, first, last):
+            if first == 0:
+                state[("planes", m)] = work.tile([P, NG, 4, 256], BF16, name="planes", tag="planes", bufs=2)
+            planes = state[("planes", m)]
+            for q in range(first, last):
+                g, t = divmod(q, 4)
+                u, e = divmod(t, 2)
+                xt = state[("xt", m, g)]
+                nc.scalar.activation(
+                    out=planes[:, g, t, :],
+                    in_=xt[:].bitcast(BF16).rearrange("p (u n e) -> p u n e", u=2, e=2)[:, u, :, e],
+                    func=COPY,
+                    scale=sc4[:, g, t : t + 1],
+                )
+
+        def x_interleave(m, g):
+            nc.scalar.copy(
+                out=xgrp[m][:, g * 1024 : (g + 1) * 1024].rearrange("p (n t) -> p n t", t=4),
+                in_=state[("planes", m)][:, g, :, :].rearrange("p t n -> p n t"),
+            )
+
+        def x_quant(m):
+            nc.vector.quantize_mx(out=xcodes[m][:].bitcast(FP8X4), scales=xscales[m][:], in_=xgrp[m][:])
+
+        def matmuls_kv(m, part):
+            ps = psum.tile([P, 512], F32, name="ps", tag="ps", bufs=6)
+            for h in range(2):
+                for j in range(NJ):
+                    for g in range(NG):
+                        cols = slice((2 * g + j) * P, (2 * g + j + 1) * P)
+                        wcols = slice(part * 256 + h * DH, part * 256 + (h + 1) * DH)
+                        nc.tensor.matmul_mx(
+                            out=ps[:, (2 * h + j) * DH : (2 * h + j + 1) * DH],
+                            lhsT=xcodes[m][:, cols].bitcast(FP8X4),
+                            lhsT_scale=xscales[m][:, cols],
+                            rhs=wcodes[2][:, g, wcols].bitcast(FP8X4),
+                            rhs_scale=wscales[2][:, g, wcols],
+                            start=(g == 0),
+                            stop=(g == NG - 1),
+                        )
+            state[("ps", m, 2, part)] = ps
+
+        def rope_k(m):
+            ps = state[("ps", m, 2, 0)]
+            res = work.tile([P, 2, NJ, DH], F32, name="res2", tag="res2", bufs=3)
+            tcos = work.tile([P, 512], F32, name="tcos", tag="tcos", bufs=6)
+            tsin = work.tile([P, 512], F32, name="tsin", tag="tsin", bufs=6)
+            u = ps[:].rearrange("p (h n e) -> p h n e", h=2, e=2)
+            cosb = cos_t[:, m, :].unsqueeze(1).unsqueeze(3).to_broadcast([P, 2, NJ * 64, 2])
+            sinb = sin2[:, m, :, :].unsqueeze(1).to_broadcast([P, 2, NJ * 64, 2])
+            nc.vector.tensor_tensor(out=tcos[:].rearrange("p (h n e) -> p h n e", h=2, e=2), in0=u, in1=cosb, op=MULT)
+            nc.vector.tensor_tensor(
+                out=tsin[:].rearrange("p (h n e) -> p h n e", h=2, e=2), in0=u[:, :, :, ::-1], in1=sinb, op=MULT
+            )
+            add_engine = nc.vector if (m, 2, 0) in V_ADD else nc.gpsimd
+            add_engine.tensor_tensor(out=res[:].rearrange("p h j d -> p (h j d)"), in0=tcos[:], in1=tsin[:], op=ADD)
+            nc.sync.dma_start(out=k_view[m], in_=res[:].rearrange("p h j d -> p h (j d)"))
+
+        def copy_v(m):
+            resv = work.tile([P, 2, NJ, DH], F32, name="resv", tag="resv", bufs=3)
+            nc.scalar.copy(out=resv[:].rearrange("p h j d -> p (h j d)"), in_=state[("ps", m, 2, 1)][:])
+            nc.sync.dma_start(out=v_view[m], in_=resv[:].rearrange("p h j d -> p h (j d)"))
+
+        def matmuls(m, c, j):
+            if c == 2:
+                matmuls_kv(m, j)
+                return
+            ps = psum.tile([P, 512], F32, name="ps", tag="ps", bufs=6)
+            for g in range(NG):
+                cols = slice((2 * g + j) * P, (2 * g + j + 1) * P)
+                nc.tensor.matmul_mx(
+                    out=ps[:],
+                    lhsT=xcodes[m][:, cols].bitcast(FP8X4),
+                    lhsT_scale=xscales[m][:, cols],
+                    rhs=wcodes[c][:, g, :].bitcast(FP8X4),
+                    rhs_scale=wscales[c][:, g, :],
+                    start=(g == 0),
+                    stop=(g == NG - 1),
+                )
+            state[("ps", m, c, j)] = ps
+
+        def rope(m, c, j):
+            if c == 2 and j == 0:
+                rope_k(m)
+                return
+            if c == 2:
+                copy_v(m)
+                return
+            ps = state[("ps", m, c, j)]
+            nh = 4 if c < 2 else 2
+            if j == 0:
+                state[("res", m, c)] = work.tile([P, nh, NJ, DH], F32, name="res%d" % nh, tag="res%d" % nh, bufs=4)
+                if c == 2:
+                    state[("resv", m)] = work.tile([P, 2, NJ, DH], F32, name="resv", tag="resv", bufs=3)
+            res = state[("res", m, c)]
+            tcos = work.tile([P, 512], F32, name="tcos", tag="tcos", bufs=6)
+            tsin = work.tile([P, 512], F32, name="tsin", tag="tsin", bufs=6)
+            w = nh * DH
+            u = ps[:, 0:w].rearrange("p (h i e) -> p h i e", h=nh, e=2)
+            cosb = cos_t[:, m, j * 64 : (j + 1) * 64].unsqueeze(1).unsqueeze(3).to_broadcast([P, nh, 64, 2])
+            sinb = sin2[:, m, j * 64 : (j + 1) * 64, :].unsqueeze(1).to_broadcast([P, nh, 64, 2])
+            nc.vector.tensor_tensor(
+                out=tcos[:, 0:w].rearrange("p (h i e) -> p h i e", h=nh, e=2), in0=u, in1=cosb, op=MULT
+            )
+            nc.vector.tensor_tensor(
+                out=tsin[:, 0:w].rearrange("p (h i e) -> p h i e", h=nh, e=2), in0=u[:, :, :, ::-1], in1=sinb, op=MULT
+            )
+            if c == 2:
+                nc.scalar.copy(
+                    out=state[("resv", m)][:, :, j, :], in_=ps[:, 256:512].rearrange("p (h d) -> p h d", h=2)
+                )
+            add_engine = nc.vector if (m, c, j) in V_ADD else nc.gpsimd
+            add_engine.tensor_tensor(
+                out=res[:, :, j, :],
+                in0=tcos[:, 0:w].rearrange("p (h d) -> p h d", h=nh),
+                in1=tsin[:, 0:w].rearrange("p (h d) -> p h d", h=nh),
+                op=ADD,
+            )
+            if j == NJ - 1:
+                flat = res[:].rearrange("p h j d -> p h (j d)")
+                if c < 2:
+                    nc.sync.dma_start(out=q_view[m][:, 4 * c : 4 * c + 4, :], in_=flat)
+                else:
+                    nc.sync.dma_start(out=k_view[m], in_=flat)
+                    nc.sync.dma_start(out=v_view[m], in_=state[("resv", m)][:].rearrange("p h j d -> p h (j d)"))
+
+        events = {}
+
+        def at(s, fn, *args):
+            events.setdefault(s, []).append((fn, args))
+
+        at(-20, w_interleave, 0, 0, "g")
+        at(-20, w_interleave, 0, 1, "g")
+        at(-20, sin2_build)
+        at(-19, x_cast, 0, 0, 0, 512)
+        at(-19, x_cast, 0, 1, 0, 512)
+        at(-19, x_cast, 0, 0, 512, D)
+        at(-19, x_cast, 0, 1, 512, D)
+        at(-18, x_transpose, 0)
+        at(-17, x_cast, 1, 0)
+        at(-17, x_cast, 1, 1)
+        at(-16, x_scale_v, 0, 0)
+        at(-16, x_scale_v, 0, 1)
+        at(-15, x_transpose, 1)
+        at(-14, x_scale_v, 1, 0)
+        at(-14, x_scale_v, 1, 1)
+        at(-13, w_interleave, 1, 0, "s")
+        at(-13, w_interleave, 1, 1, "s")
+        at(-12, x_quant, 0)
+        at(-12, w_quant, 0)
+        at(-12, x_quant, 1)
+        at(-11, x_cast, 2, 0)
+        at(-11, x_cast, 2, 1)
+        at(-10, w_interleave, 2, 0, "s")
+        at(-10, w_interleave, 2, 1, "s")
+        at(-9, x_cast, 3, 0)
+        at(-9, x_cast, 3, 1)
+        at(-8, x_cast, 5, 0)
+        at(-8, x_cast, 5, 1)
+        at(-1, x_transpose, 2)
+        at(0, w_quant, 1)
+        at(1, x_scale_v, 2, 0)
+        at(2, x_scale_v, 2, 1)
+        at(4, w_quant, 2)
+        at(5, x_quant, 2)
+        at(5, x_transpose, 3)
+        at(6, x_scale_v, 3, 0)
+        at(7, x_scale_v, 3, 1)
+        at(8, x_transpose, 5)
+        at(8, x_cast, 4, 0)
+        at(8, x_cast, 4, 1)
+        at(9, x_planes, 5, 0, 3)
+        at(10, x_quant, 3)
+        at(10, x_planes, 5, 3, 6)
+        at(11, x_planes, 5, 6, 8)
+        at(12, x_interleave, 5, 0)
+        at(13, x_interleave, 5, 1)
+        at(13, x_transpose, 4)
+        at(14, x_scale_v, 4, 0)
+        at(14, x_cast, 6, 0)
+        at(15, x_scale_v, 4, 1)
+        at(15, x_cast, 6, 1)
+        at(16, x_transpose, 6)
+        at(16, x_cast, 7, 0)
+        at(17, x_cast, 7, 1)
+        at(18, x_quant, 4)
+        at(18, x_planes, 6, 0, 3)
+        at(19, x_planes, 6, 3, 6)
+        at(20, x_planes, 6, 6, 8)
+        at(21, x_transpose, 7)
+        at(24, x_interleave, 6, 0)
+        at(24, x_interleave, 6, 1)
+        at(24, x_quant, 5)
+        at(25, x_planes, 7, 0, 3)
+        at(26, x_planes, 7, 3, 6)
+        at(27, x_planes, 7, 6, 8)
+        at(30, x_interleave, 7, 0)
+        at(30, x_interleave, 7, 1)
+        at(30, x_quant, 6)
+        at(36, x_quant, 7)
+
+        units = [(m, c, j) for c in range(NC) for m in range(2) for j in range(NJ)]
+        units.extend([(m, c, j) for m in range(2, NB) for c in range(NC) for j in range(NJ)])
+
+        for s in range(-20, len(units)):
+            tau = s + LOOK
+            if 0 <= tau < len(units):
+                matmuls(*units[tau])
+            if s >= 0:
+                rope(*units[s])
+            for fn, args in events.get(s, []):
+                fn(*args)

@@ -22,7 +22,8 @@ NJ = 2
 NG = 2
 NC = 3
 LOOK = 3
-V_ADD = ((7, 1, 1), (7, 2, 0))
+V_ADD = ((7, 1, 1), (7, 0, 1))
+LAST = (7, 1)
 
 
 def tile_gqamultiheadattention_pa_kernel(
@@ -260,7 +261,9 @@ def tile_gqamultiheadattention_pa_kernel(
                 in1=tsin[:, 0:w].rearrange("p (h d) -> p h d", h=nh),
                 op=ADD,
             )
-            if j == NJ - 1:
+            if (m, c) == LAST:
+                nc.sync.dma_start(out=q_view[m][:, 4 * c : 4 * c + 4, j * DH : (j + 1) * DH], in_=res[:, :, j, :])
+            elif j == NJ - 1:
                 flat = res[:].rearrange("p h j d -> p h (j d)")
                 if c < 2:
                     nc.sync.dma_start(out=q_view[m][:, 4 * c : 4 * c + 4, :], in_=flat)
@@ -343,8 +346,11 @@ def tile_gqamultiheadattention_pa_kernel(
         at(30, x_quant, 6)
         at(36, x_quant, 7)
 
+
         units = [(m, c, j) for c in range(NC) for m in range(2) for j in range(NJ)]
-        units.extend([(m, c, j) for m in range(2, NB) for c in range(NC) for j in range(NJ)])
+        units.extend([(m, c, j) for m in range(2, NB - 1) for c in range(NC) for j in range(NJ)])
+        units.extend([(NB - 1, 2, 1), (NB - 1, 2, 0)])
+        units.extend([(NB - 1, c, j) for c in range(2) for j in range(NJ)])
 
         for s in range(-20, len(units)):
             tau = s + LOOK

@@ -302,50 +302,52 @@ def tile_gqamultiheadattention_pa_kernel(
         at(-10, w_interleave, 2, 1, "s")
         at(-9, x_cast, 3, 0)
         at(-9, x_cast, 3, 1)
-        at(-8, x_cast, 5, 0)
-        at(-8, x_cast, 5, 1)
         at(-1, x_transpose, 2)
         at(0, w_quant, 1)
         at(1, x_scale_v, 2, 0)
         at(2, x_scale_v, 2, 1)
         at(4, w_quant, 2)
         at(5, x_quant, 2)
+        at(-8, x_cast, 4, 0)
+        at(-8, x_cast, 4, 1)
         at(5, x_transpose, 3)
         at(6, x_scale_v, 3, 0)
         at(7, x_scale_v, 3, 1)
-        at(8, x_transpose, 5)
-        at(8, x_cast, 4, 0)
-        at(8, x_cast, 4, 1)
-        at(9, x_planes, 5, 0, 3)
         at(10, x_quant, 3)
-        at(10, x_planes, 5, 3, 6)
-        at(11, x_planes, 5, 6, 8)
-        at(12, x_interleave, 5, 0)
-        at(13, x_interleave, 5, 1)
-        at(13, x_transpose, 4)
-        at(14, x_scale_v, 4, 0)
+        at(8, x_cast, 5, 0)
+        at(8, x_cast, 5, 1)
         at(14, x_cast, 6, 0)
-        at(15, x_scale_v, 4, 1)
         at(15, x_cast, 6, 1)
-        at(16, x_transpose, 6)
-        at(16, x_cast, 7, 0)
-        at(17, x_cast, 7, 1)
+        at(20, x_cast, 7, 0)
+        at(21, x_cast, 7, 1)
+        at(8, x_transpose, 4)
+        at(8, x_planes, 4, 0, 3)
+        at(9, x_planes, 4, 3, 6)
+        at(10, x_planes, 4, 6, 8)
+        at(11, x_interleave, 4, 0)
+        at(12, x_interleave, 4, 1)
         at(18, x_quant, 4)
-        at(18, x_planes, 6, 0, 3)
-        at(19, x_planes, 6, 3, 6)
-        at(20, x_planes, 6, 6, 8)
-        at(21, x_transpose, 7)
-        at(24, x_interleave, 6, 0)
-        at(24, x_interleave, 6, 1)
+        at(14, x_transpose, 5)
+        at(14, x_planes, 5, 0, 3)
+        at(15, x_planes, 5, 3, 6)
+        at(16, x_planes, 5, 6, 8)
+        at(17, x_interleave, 5, 0)
+        at(18, x_interleave, 5, 1)
         at(24, x_quant, 5)
-        at(25, x_planes, 7, 0, 3)
-        at(26, x_planes, 7, 3, 6)
-        at(27, x_planes, 7, 6, 8)
-        at(30, x_interleave, 7, 0)
-        at(30, x_interleave, 7, 1)
+        at(20, x_transpose, 6)
+        at(20, x_planes, 6, 0, 3)
+        at(21, x_planes, 6, 3, 6)
+        at(22, x_planes, 6, 6, 8)
+        at(23, x_interleave, 6, 0)
+        at(24, x_interleave, 6, 1)
         at(30, x_quant, 6)
+        at(26, x_transpose, 7)
+        at(26, x_planes, 7, 0, 3)
+        at(27, x_planes, 7, 3, 6)
+        at(28, x_planes, 7, 6, 8)
+        at(29, x_interleave, 7, 0)
+        at(30, x_interleave, 7, 1)
         at(36, x_quant, 7)
-
 
         units = [(m, c, j) for c in range(NC) for m in range(2) for j in range(NJ)]
         units.extend([(m, c, j) for m in range(2, NB - 1) for c in range(NC) for j in range(NJ)])

@@ -23,6 +23,7 @@ NG = 2
 NC = 3
 LOOK = 3
 V_ADD = ((7, 1, 1), (7, 0, 1))
+SPLIT = tuple((m, c) for m in range(8) for c in range(2))
 LAST = (7, 1)
 
 
@@ -188,8 +189,8 @@ def tile_gqamultiheadattention_pa_kernel(
         def rope_k(m):
             ps = state[("ps", m, 2, 0)]
             res = work.tile([P, 2, NJ, DH], F32, name="res2", tag="res2", bufs=3)
-            tcos = work.tile([P, 512], F32, name="tcos", tag="tcos", bufs=6)
-            tsin = work.tile([P, 512], F32, name="tsin", tag="tsin", bufs=6)
+            tcos = work.tile([P, 512], F32, name="tcos", tag="tcos", bufs=2)
+            tsin = work.tile([P, 512], F32, name="tsin", tag="tsin", bufs=2)
             u = ps[:].rearrange("p (h n e) -> p h n e", h=2, e=2)
             cosb = cos_t[:, m, :].unsqueeze(1).unsqueeze(3).to_broadcast([P, 2, NJ * 64, 2])
             sinb = sin2[:, m, :, :].unsqueeze(1).to_broadcast([P, 2, NJ * 64, 2])
@@ -238,29 +239,30 @@ def tile_gqamultiheadattention_pa_kernel(
                 if c == 2:
                     state[("resv", m)] = work.tile([P, 2, NJ, DH], F32, name="resv", tag="resv", bufs=3)
             res = state[("res", m, c)]
-            tcos = work.tile([P, 512], F32, name="tcos", tag="tcos", bufs=6)
-            tsin = work.tile([P, 512], F32, name="tsin", tag="tsin", bufs=6)
-            w = nh * DH
-            u = ps[:, 0:w].rearrange("p (h i e) -> p h i e", h=nh, e=2)
-            cosb = cos_t[:, m, j * 64 : (j + 1) * 64].unsqueeze(1).unsqueeze(3).to_broadcast([P, nh, 64, 2])
-            sinb = sin2[:, m, j * 64 : (j + 1) * 64, :].unsqueeze(1).to_broadcast([P, nh, 64, 2])
+            if j == 0:
+                state[("tc", m, c)] = work.tile([P, 4, NJ, DH], F32, name="tcos4", tag="tcos4", bufs=3)
+                state[("ts", m, c)] = work.tile([P, 4, NJ, DH], F32, name="tsin4", tag="tsin4", bufs=3)
+            tcos = state[("tc", m, c)]
+            tsin = state[("ts", m, c)]
+            u = ps[:].rearrange("p (h i e) -> p h i e", h=4, e=2)
+            cosb = cos_t[:, m, j * 64 : (j + 1) * 64].unsqueeze(1).unsqueeze(3).to_broadcast([P, 4, 64, 2])
+            sinb = sin2[:, m, j * 64 : (j + 1) * 64, :].unsqueeze(1).to_broadcast([P, 4, 64, 2])
             nc.vector.tensor_tensor(
-                out=tcos[:, 0:w].rearrange("p (h i e) -> p h i e", h=nh, e=2), in0=u, in1=cosb, op=MULT
+                out=tcos[:, :, j, :].rearrange("p h (i e) -> p h i e", e=2), in0=u, in1=cosb, op=MULT
             )
             nc.vector.tensor_tensor(
-                out=tsin[:, 0:w].rearrange("p (h i e) -> p h i e", h=nh, e=2), in0=u[:, :, :, ::-1], in1=sinb, op=MULT
+                out=tsin[:, :, j, :].rearrange("p h (i e) -> p h i e", e=2), in0=u[:, :, :, ::-1], in1=sinb, op=MULT
             )
-            if c == 2:
-                nc.scalar.copy(
-                    out=state[("resv", m)][:, :, j, :], in_=ps[:, 256:512].rearrange("p (h d) -> p h d", h=2)
+            if (m, c) in SPLIT:
+                add_engine = nc.vector if (m, c, j) in V_ADD else nc.gpsimd
+                add_engine.tensor_tensor(out=res[:, :, j, :], in0=tcos[:, :, j, :], in1=tsin[:, :, j, :], op=ADD)
+            elif j == NJ - 1:
+                nc.gpsimd.tensor_tensor(
+                    out=res[:].rearrange("p h j d -> p (h j d)"),
+                    in0=tcos[:].rearrange("p h j d -> p (h j d)"),
+                    in1=tsin[:].rearrange("p h j d -> p (h j d)"),
+                    op=ADD,
                 )
-            add_engine = nc.vector if (m, c, j) in V_ADD else nc.gpsimd
-            add_engine.tensor_tensor(
-                out=res[:, :, j, :],
-                in0=tcos[:, 0:w].rearrange("p (h d) -> p h d", h=nh),
-                in1=tsin[:, 0:w].rearrange("p (h d) -> p h d", h=nh),
-                op=ADD,
-            )
             if (m, c) == LAST:
                 nc.sync.dma_start(out=q_view[m][:, 4 * c : 4 * c + 4, j * DH : (j + 1) * DH], in_=res[:, :, j, :])
             elif j == NJ - 1:

@@ -93,8 +93,8 @@ def tile_gqamultiheadattention_pa_kernel(
         state = {}
 
         def w_interleave(c, g, eng):
-            dst = wgrp[c][:, g, :, :]
-            src = wraw[(g, c)][:].rearrange("p j n -> p n j")
+            dst = wgrp[c][:, g, :, :].rearrange("p (c i) j -> p c j i", i=4)
+            src = wraw[(g, c)][:].rearrange("p j (c i) -> p c j i", i=4)
             if eng == "g":
                 nc.gpsimd.tensor_scalar(out=dst, in0=src, scalar1=1.0, scalar2=0.0, op0=MULT, op1=ADD)
             else:
@@ -161,8 +161,8 @@ def tile_gqamultiheadattention_pa_kernel(
 
         def x_interleave(m, g):
             nc.scalar.copy(
-                out=xgrp[m][:, g * 1024 : (g + 1) * 1024].rearrange("p (n t) -> p n t", t=4),
-                in_=state[("planes", m)][:, g, :, :].rearrange("p t n -> p n t"),
+                out=xgrp[m][:, g * 1024 : (g + 1) * 1024].rearrange("p (c i t) -> p c t i", i=4, t=4),
+                in_=state[("planes", m)][:, g, :, :].rearrange("p t (c i) -> p c t i", i=4),
             )
 
         def x_quant(m):

@@ -306,15 +306,15 @@ def tile_gqamultiheadattention_pa_kernel(
         at(-9, x_cast, 3, 1)
         at(-1, x_transpose, 2)
         at(0, w_quant, 1)
-        at(1, x_scale_v, 2, 0)
-        at(2, x_scale_v, 2, 1)
-        at(4, w_quant, 2)
-        at(5, x_quant, 2)
+        at(3, x_scale_v, 2, 0)
+        at(3, x_scale_v, 2, 1)
+        at(3, w_quant, 2)
         at(-8, x_cast, 4, 0)
         at(-8, x_cast, 4, 1)
         at(5, x_transpose, 3)
-        at(6, x_scale_v, 3, 0)
+        at(7, x_scale_v, 3, 0)
         at(7, x_scale_v, 3, 1)
+        at(7, x_quant, 2)
         at(10, x_quant, 3)
         at(8, x_cast, 5, 0)
         at(8, x_cast, 5, 1)

from contextlib import ExitStack

import concourse.masks as masks
import concourse.mybir as mybir

F32 = mybir.dt.float32
BF16 = mybir.dt.bfloat16
U32 = mybir.dt.uint32
U8 = mybir.dt.uint8
FP8 = mybir.dt.float8_e4m3fn
FP8X4 = mybir.dt.float8_e4m3fn_x4
MULT = mybir.AluOpType.mult
ADD = mybir.AluOpType.add
COPY = mybir.ActivationFunctionType.Copy

T, D, DH = 2048, 1024, 128
FLOPS = 2 * T * D * 1536

P = 128
NB = 8
NJ = 2
NG = 2
NC = 3
LOOK = 3
V_ADD = ((7, 1, 1), (7, 0, 1))
SPLIT = tuple((m, c) for m in range(8) for c in range(2))
LAST = (7, 1)


def tile_gqamultiheadattention_pa_kernel(
    tc, x_bytes, x_scale, Wq, Wk, Wv, rope_sin, rope_cos, out_0, out_1, out_2
):
    nc = tc.nc
    with ExitStack() as ctx:
        keep = ctx.enter_context(tc.tile_pool(name="keep", bufs=1))
        work = ctx.enter_context(tc.tile_pool(name="work", bufs=2))
        psum = ctx.enter_context(tc.psum_pool(name="psum", bufs=2))
        ctx.enter_context(tc.manual_schedule())

        xb_view = x_bytes[0].rearrange("(b p j) k -> b p (j k)", p=P, j=NJ)
        sc_view = x_scale[0, 0].rearrange("(g p t) -> p g t", p=P, t=4)
        wq_view = Wq.rearrange("(g p j) n -> g p j n", p=P, j=4)
        wk_view = Wk.rearrange("(g p j) n -> g p j n", p=P, j=4)
        wv_view = Wv.rearrange("(g p j) n -> g p j n", p=P, j=4)
        sin_view = rope_sin.rearrange("(b p j) i -> p b (j i)", p=P, j=NJ)
        cos_view = rope_cos.rearrange("(b p j) i -> p b (j i)", p=P, j=NJ)
        q_view = out_0[0].rearrange("h (b p j) d -> b p h (j d)", p=P, j=NJ)
        k_view = out_1[0].rearrange("h (b p j) d -> b p h (j d)", p=P, j=NJ)
        v_view = out_2[0].rearrange("h (b p j) d -> b p h (j d)", p=P, j=NJ)

        xbytes = [keep.tile([P, NJ * D], U8, name="xbytes%d" % m) for m in range(NB)]
        sc4 = keep.tile([P, NG, 4], F32, name="sc4")
        wraw = {}
        for c in range(NC):
            for g in range(NG):
                wraw[(g, c)] = keep.tile([P, 4, 512], BF16, name="wraw%d%d" % (g, c))
        wgrp = [keep.tile([P, NG, 512, 4], BF16, name="wgrp%d" % c, align_bytes=64) for c in range(NC)]
        wcodes = [keep.tile([P, NG, 512], U32, name="wcodes%d" % c, align_bytes=64) for c in range(NC)]
        wscales = [keep.tile([P, NG, 512], U8, name="wscales%d" % c, align_bytes=64) for c in range(NC)]
        xgrp = [keep.tile([P, NG * NJ * P * 4], BF16, name="xgrp%d" % m, align_bytes=64) for m in range(NB)]
        xcodes = [keep.tile([P, NG * NJ * P], U32, name="xcodes%d" % m, align_bytes=64) for m in range(NB)]
        xscales = [keep.tile([P, NG * NJ * P], U8, name="xscales%d" % m, align_bytes=64) for m in range(NB)]
        sin_t = keep.tile([P, NB, NJ * 64], BF16, name="sin_t")
        cos_t = keep.tile([P, NB, NJ * 64], BF16, name="cos_t")
        sin2 = keep.tile([P, NB, NJ * 64, 2], BF16, name="sin2")
        sgn = keep.tile([P, 2], BF16, name="sgn")
        ident = keep.tile([P, P], F32, name="ident")
        warm_in = keep.tile([P, 1], F32, name="warm_in")
        warm_out = keep.tile([P, 1], F32, name="warm_out")

        nc.sync.dma_start(out=xbytes[0][:], in_=xb_view[0])
        nc.sync.dma_start(out=sin_t[:], in_=sin_view)
        nc.sync.dma_start(out=sc4[:], in_=sc_view)
        nc.sync.dma_start(out=xbytes[1][:], in_=xb_view[1])
        for g in range(NG):
            nc.sync.dma_start(out=wraw[(g, 0)][:], in_=wq_view[g][:, :, 0:512])
        nc.sync.dma_start(out=cos_t[:], in_=cos_view)
        for g in range(NG):
            nc.sync.dma_start(out=wraw[(g, 1)][:], in_=wq_view[g][:, :, 512:1024])
        nc.sync.dma_start(out=xbytes[2][:], in_=xb_view[2])
        for g in range(NG):
            nc.sync.dma_start(out=wraw[(g, 2)][:, :, 0:256], in_=wk_view[g])
            nc.sync.dma_start(out=wraw[(g, 2)][:, :, 256:512], in_=wv_view[g])
        for m in range(3, NB):
            nc.sync.dma_start(out=xbytes[m][:], in_=xb_view[m])

        nc.vector.memset(warm_in[:], 0.0)
        nc.vector.memset(sgn[:, 0:1], -1.0)
        nc.vector.memset(sgn[:, 1:2], 1.0)
        nc.scalar.copy(out=warm_out[:], in_=warm_in[:])
        masks.make_identity(nc, ident[:])

        state = {}

        def w_interleave(c, g, eng):
            dst = wgrp[c][:, g, :, :].rearrange("p (c i) j -> p c j i", i=4)
            src = wraw[(g, c)][:].rearrange("p j (c i) -> p c j i", i=4)
            if eng == "g":
                nc.gpsimd.tensor_scalar(out=dst, in0=src, scalar1=1.0, scalar2=0.0, op0=MULT, op1=ADD)
            else:
                nc.scalar.copy(out=dst, in_=src)

        def w_quant(c):
            nc.vector.quantize_mx(
                out=wcodes[c][:].rearrange("p g n -> p (g n)").bitcast(FP8X4),
                scales=wscales[c][:].rearrange("p g n -> p (g n)"),
                in_=wgrp[c][:].rearrange("p g n j -> p (g n j)"),
            )

        def sin2_build():
            n = NB * NJ * 64
            nc.vector.tensor_tensor(
                out=sin2[:].rearrange("p b n e -> p (b n) e"),
                in0=sin_t[:].rearrange("p b n -> p (b n)").unsqueeze(2).to_broadcast([P, n, 2]),
                in1=sgn[:].unsqueeze(1).to_broadcast([P, n, 2]),
                op=MULT,
            )

        def x_cast(m, j, first=0, last=D):
            if first == 0:
                state[("xbf", m, j)] = work.tile([P, D], BF16, name="xbf", tag="xbf", bufs=6, align_bytes=64)
            nc.scalar.copy(
                out=state[("xbf", m, j)][:, first:last], in_=xbytes[m][:, j * D + first : j * D + last].bitcast(FP8)
            )

        def x_transpose(m):
            for g in range(NG):
                xt = psum.tile([P, 512], F32, name="xt", tag="xt", bufs=2)
                for u in range(2):
                    for j in range(NJ):
                        s = 2 * u + j
                        words = state[("xbf", m, j)][:].bitcast(F32)
                        nc.tensor.transpose(
                            xt[:, s * P : (s + 1) * P], words[:, 256 * g + u : 256 * (g + 1) : 2], ident[:]
                        )
                state[("xt", m, g)] = xt

        def x_scale_v(m, g):
            xt = state[("xt", m, g)]
            nc.vector.tensor_tensor(
                out=xgrp[m][:, g * 1024 : (g + 1) * 1024].rearrange("p (n u e) -> p n u e", u=2, e=2),
                in0=xt[:].bitcast(BF16).rearrange("p (u n e) -> p n u e", u=2, e=2),
                in1=sc4[:, g, :].rearrange("p (u e) -> p u e", e=2).unsqueeze(1).to_broadcast([P, 256, 2, 2]),
                op=MULT,
            )

        def x_planes(m, first, last):
            if first == 0:
                state[("planes", m)] = work.tile([P, NG, 4, 256], BF16, name="planes", tag="planes", bufs=2)
            planes = state[("planes", m)]
            for q in range(first, last):
                g, t = divmod(q, 4)
                u, e = divmod(t, 2)
                xt = state[("xt", m, g)]
                nc.scalar.activation(
                    out=planes[:, g, t, :],
                    in_=xt[:].bitcast(BF16).rearrange("p (u n e) -> p u n e", u=2, e=2)[:, u, :, e],
                    func=COPY,
                    scale=sc4[:, g, t : t + 1],
                )

        def x_interleave(m, g):
            nc.scalar.copy(
                out=xgrp[m][:, g * 1024 : (g + 1) * 1024].rearrange("p (c i t) -> p c t i", i=4, t=4),
                in_=state[("planes", m)][:, g, :, :].rearrange("p t (c i) -> p c t i", i=4),
            )

        def x_quant(m):
            nc.vector.quantize_mx(out=xcodes[m][:].bitcast(FP8X4), scales=xscales[m][:], in_=xgrp[m][:])

        def matmuls_kv(m, part):
            ps = psum.tile([P, 512], F32, name="ps", tag="ps", bufs=6)
            for h in range(2):
                for j in range(NJ):
                    for g in range(NG):
                        cols = slice((2 * g + j) * P, (2 * g + j + 1) * P)
                        wcols = slice(part * 256 + h * DH, part * 256 + (h + 1) * DH)
                        nc.tensor.matmul_mx(
                            out=ps[:, (2 * h + j) * DH : (2 * h + j + 1) * DH],
                            lhsT=xcodes[m][:, cols].bitcast(FP8X4),
                            lhsT_scale=xscales[m][:, cols],
                            rhs=wcodes[2][:, g, wcols].bitcast(FP8X4),
                            rhs_scale=wscales[2][:, g, wcols],
                            start=(g == 0),
                            stop=(g == NG - 1),
                        )
            state[("ps", m, 2, part)] = ps

        def rope_k(m):
            ps = state[("ps", m, 2, 0)]
            res = work.tile([P, 2, NJ, DH], F32, name="res2", tag="res2", bufs=3)
            tcos = work.tile([P, 512], F32, name="tcos", tag="tcos", bufs=2)
            tsin = work.tile([P, 512], F32, name="tsin", tag="tsin", bufs=2)
            u = ps[:].rearrange("p (h n e) -> p h n e", h=2, e=2)
            cosb = cos_t[:, m, :].unsqueeze(1).unsqueeze(3).to_broadcast([P, 2, NJ * 64, 2])
            sinb = sin2[:, m, :, :].unsqueeze(1).to_broadcast([P, 2, NJ * 64, 2])
            nc.vector.tensor_tensor(out=tcos[:].rearrange("p (h n e) -> p h n e", h=2, e=2), in0=u, in1=cosb, op=MULT)
            nc.vector.tensor_tensor(
                out=tsin[:].rearrange("p (h n e) -> p h n e", h=2, e=2), in0=u[:, :, :, ::-1], in1=sinb, op=MULT
            )
            add_engine = nc.vector if (m, 2, 0) in V_ADD else nc.gpsimd
            add_engine.tensor_tensor(out=res[:].rearrange("p h j d -> p (h j d)"), in0=tcos[:], in1=tsin[:], op=ADD)
            nc.sync.dma_start(out=k_view[m], in_=res[:].rearrange("p h j d -> p h (j d)"))

        def copy_v(m):
            resv = work.tile([P, 2, NJ, DH], F32, name="resv", tag="resv", bufs=3)
            nc.scalar.copy(out=resv[:].rearrange("p h j d -> p (h j d)"), in_=state[("ps", m, 2, 1)][:])
            nc.sync.dma_start(out=v_view[m], in_=resv[:].rearrange("p h j d -> p h (j d)"))

        def matmuls(m, c, j):
            if c == 2:
                matmuls_kv(m, j)
                return
            ps = psum.tile([P, 512], F32, name="ps", tag="ps", bufs=6)
            for g in range(NG):
                cols = slice((2 * g + j) * P, (2 * g + j + 1) * P)
                nc.tensor.matmul_mx(
                    out=ps[:],
                    lhsT=xcodes[m][:, cols].bitcast(FP8X4),
                    lhsT_scale=xscales[m][:, cols],
                    rhs=wcodes[c][:, g, :].bitcast(FP8X4),
                    rhs_scale=wscales[c][:, g, :],
                    start=(g == 0),
                    stop=(g == NG - 1),
                )
            state[("ps", m, c, j)] = ps

        def rope(m, c, j):
            if c == 2 and j == 0:
                rope_k(m)
                return
            if c == 2:
                copy_v(m)
                return
            ps = state[("ps", m, c, j)]
            nh = 4 if c < 2 else 2
            if j == 0:
                state[("res", m, c)] = work.tile([P, nh, NJ, DH], F32, name="res%d" % nh, tag="res%d" % nh, bufs=4)
                if c == 2:
                    state[("resv", m)] = work.tile([P, 2, NJ, DH], F32, name="resv", tag="resv", bufs=3)
            res = state[("res", m, c)]
            if j == 0:
                state[("tc", m, c)] = work.tile([P, 4, NJ, DH], F32, name="tcos4", tag="tcos4", bufs=3)
                state[("ts", m, c)] = work.tile([P, 4, NJ, DH], F32, name="tsin4", tag="tsin4", bufs=3)
            tcos = state[("tc", m, c)]
            tsin = state[("ts", m, c)]
            u = ps[:].rearrange("p (h i e) -> p h i e", h=4, e=2)
            cosb = cos_t[:, m, j * 64 : (j + 1) * 64].unsqueeze(1).unsqueeze(3).to_broadcast([P, 4, 64, 2])
            sinb = sin2[:, m, j * 64 : (j + 1) * 64, :].unsqueeze(1).to_broadcast([P, 4, 64, 2])
            nc.vector.tensor_tensor(
                out=tcos[:, :, j, :].rearrange("p h (i e) -> p h i e", e=2), in0=u, in1=cosb, op=MULT
            )
            nc.vector.tensor_tensor(
                out=tsin[:, :, j, :].rearrange("p h (i e) -> p h i e", e=2), in0=u[:, :, :, ::-1], in1=sinb, op=MULT
            )
            if (m, c) in SPLIT:
                add_engine = nc.vector if (m, c, j) in V_ADD else nc.gpsimd
                add_engine.tensor_tensor(out=res[:, :, j, :], in0=tcos[:, :, j, :], in1=tsin[:, :, j, :], op=ADD)
            elif j == NJ - 1:
                nc.gpsimd.tensor_tensor(
                    out=res[:].rearrange("p h j d -> p (h j d)"),
                    in0=tcos[:].rearrange("p h j d -> p (h j d)"),
                    in1=tsin[:].rearrange("p h j d -> p (h j d)"),
                    op=ADD,
                )
            if (m, c) == LAST:
                nc.sync.dma_start(out=q_view[m][:, 4 * c : 4 * c + 4, j * DH : (j + 1) * DH], in_=res[:, :, j, :])
            elif j == NJ - 1:
                flat = res[:].rearrange("p h j d -> p h (j d)")
                if c < 2:
                    nc.sync.dma_start(out=q_view[m][:, 4 * c : 4 * c + 4, :], in_=flat)
                else:
                    nc.sync.dma_start(out=k_view[m], in_=flat)
                    nc.sync.dma_start(out=v_view[m], in_=state[("resv", m)][:].rearrange("p h j d -> p h (j d)"))

        events = {}

        def at(s, fn, *args):
            events.setdefault(s, []).append((fn, args))

        at(-20, w_interleave, 0, 0, "g")
        at(-20, w_interleave, 0, 1, "g")
        at(-20, sin2_build)
        at(-19, x_cast, 0, 0, 0, 512)
        at(-19, x_cast, 0, 1, 0, 512)
        at(-19, x_cast, 0, 0, 512, D)
        at(-19, x_cast, 0, 1, 512, D)
        at(-18, x_transpose, 0)
        at(-17, x_cast, 1, 0)
        at(-17, x_cast, 1, 1)
        at(-16, x_scale_v, 0, 0)
        at(-16, x_scale_v, 0, 1)
        at(-15, x_transpose, 1)
        at(-14, x_scale_v, 1, 0)
        at(-14, x_scale_v, 1, 1)
        at(-13, w_interleave, 1, 0, "s")
        at(-13, w_interleave, 1, 1, "s")
        at(-12, x_quant, 0)
        at(-12, w_quant, 0)
        at(-12, x_quant, 1)
        at(-11, x_cast, 2, 0)
        at(-11, x_cast, 2, 1)
        at(-10, w_interleave, 2, 0, "s")
        at(-10, w_interleave, 2, 1, "s")
        at(-9, x_cast, 3, 0)
        at(-9, x_cast, 3, 1)
        at(-1, x_transpose, 2)
        at(0, w_quant, 1)
        at(3, x_scale_v, 2, 0)
        at(3, x_scale_v, 2, 1)
        at(3, w_quant, 2)
        at(-8, x_cast, 4, 0)
        at(-8, x_cast, 4, 1)
        at(5, x_transpose, 3)
        at(7, x_scale_v, 3, 0)
        at(7, x_scale_v, 3, 1)
        at(7, x_quant, 2)
        at(10, x_quant, 3)
        at(8, x_cast, 5, 0)
        at(8, x_cast, 5, 1)
        at(14, x_cast, 6, 0)
        at(15, x_cast, 6, 1)
        at(20, x_cast, 7, 0)
        at(21, x_cast, 7, 1)
        at(8, x_transpose, 4)
        at(8, x_planes, 4, 0, 3)
        at(9, x_planes, 4, 3, 6)
        at(10, x_planes, 4, 6, 8)
        at(11, x_interleave, 4, 0)
        at(12, x_interleave, 4, 1)
        at(18, x_quant, 4)
        at(14, x_transpose, 5)
        at(14, x_planes, 5, 0, 3)
        at(15, x_planes, 5, 3, 6)
        at(16, x_planes, 5, 6, 8)
        at(17, x_interleave, 5, 0)
        at(18, x_interleave, 5, 1)
        at(24, x_quant, 5)
        at(20, x_transpose, 6)
        at(20, x_planes, 6, 0, 3)
        at(21, x_planes, 6, 3, 6)
        at(22, x_planes, 6, 6, 8)
        at(23, x_interleave, 6, 0)
        at(24, x_interleave, 6, 1)
        at(30, x_quant, 6)
        at(26, x_transpose, 7)
        at(26, x_planes, 7, 0, 3)
        at(27, x_planes, 7, 3, 6)
        at(28, x_planes, 7, 6, 8)
        at(29, x_interleave, 7, 0)
        at(30, x_interleave, 7, 1)
        at(36, x_quant, 7)

        units = [(m, c, j) for c in range(NC) for m in range(2) for j in range(NJ)]
        units.extend([(m, c, j) for m in range(2, NB - 1) for c in range(NC) for j in range(NJ)])
        units.extend([(NB - 1, 2, 1), (NB - 1, 2, 0)])
        units.extend([(NB - 1, c, j) for c in range(2) for j in range(NJ)])

        for s in range(-20, len(units)):
            tau = s + LOOK
            if 0 <= tau < len(units):
                matmuls(*units[tau])
            if s >= 0:
                rope(*units[s])
            for fn, args in events.get(s, []):
                fn(*args)
